import numpy as np
import ml_dtypes


def mxq(x, axis, fmt="e4m3"):
    dtype, down = {"e4m3": (ml_dtypes.float8_e4m3fn, 7), "e5m2": (ml_dtypes.float8_e5m2, 14)}[fmt]
    v = np.moveaxis(np.asarray(x, np.float32).astype(ml_dtypes.bfloat16).astype(np.float64), axis, -1)
    blocks = v.reshape(v.shape[:-1] + (-1, 32))
    amax = np.abs(blocks).max(-1, keepdims=True)
    byte = np.maximum(np.where(amax > 0, np.frexp(amax)[1] - 1 + 127, 0) - down, 1)
    scale = np.exp2(byte - 127.0)
    codes = (blocks / scale).astype(np.float32).astype(dtype).astype(np.float64)
    return np.moveaxis((codes * scale).reshape(v.shape), -1, axis)


WIDE = False


def mx_kscale(k):
    if not WIDE:
        return np.ones(k)
    levels = np.array([10, -10, 5, -5, 0])
    a = np.random.permutation(np.resize(levels, k // 512 * 4)).reshape(k // 512, 4)
    idx = np.arange(k)
    return np.exp2(a[idx // 512, idx % 128 // 32])


BF16 = ml_dtypes.bfloat16


def bf(x):
    return np.asarray(x, np.float32).astype(BF16)


def f64(x):
    return np.asarray(x).astype(np.float64)


E2M1 = np.array([0.0, 0.5, 1.0, 1.5, 2.0, 3.0, 4.0, 6.0, -0.0, -0.5, -1.0, -1.5, -2.0, -3.0, -4.0, -6.0])


def pack_weight(w, fmt):
    k, n = w.shape
    w = f64(bf(w)).reshape(k // 32, 32, n)
    amax = np.abs(w).max(1)
    if fmt == "e4m3":
        byte = np.frexp(amax)[1] - 1 + 127 - 7
    else:
        mant, ex = np.frexp(amax / 6.0)
        byte = np.where(mant > 0.5, ex, ex - 1) + 127
    byte = np.clip(np.where(amax > 0, byte, 1), 1, 254)
    scaled = (w * np.exp2(127.0 - byte)[:, None, :]).reshape(k, n).astype(np.float32)
    by_word = np.ascontiguousarray(scaled.reshape(k // 512, 128, 4, n).transpose(0, 1, 3, 2))
    if fmt == "e4m3":
        words = by_word.astype(ml_dtypes.float8_e4m3fn).view(np.uint8)
    else:
        c = by_word.astype(ml_dtypes.float4_e2m1fn).view(np.uint8) & 0xF
        words = c[..., 0::2] | (c[..., 1::2] << 4)
    return np.ascontiguousarray(words), np.ascontiguousarray(byte.astype(np.uint8).reshape(k // 512, 16, n))


def unpack_weight(words, scales, fmt):
    g, p, n, _ = words.shape
    if fmt == "e4m3":
        vals = np.ascontiguousarray(words).view(ml_dtypes.float8_e4m3fn).astype(np.float64)
    else:
        nib = np.empty((g, p, n, 4), np.uint8)
        nib[..., 0::2] = words & 0xF
        nib[..., 1::2] = words >> 4
        vals = E2M1[nib]
    vals = vals * np.repeat(np.exp2(scales.astype(np.float64) - 127.0), 8, axis=1)[..., None]
    return vals.transpose(0, 1, 3, 2).reshape(g * 512, n)


B, IN_DIM, HID, ATT = 128, 512, 2048, 1536
TOTAL = IN_DIM + HID + ATT


def softplus(v):
    return np.logaddexp(v, 0.0)


def sigmoid(v):
    return 1.0 / (1.0 + np.exp(-v))


def setup_inputs():
    s = np.array(mx_kscale(TOTAL), np.float64)
    s[IN_DIM:IN_DIM + HID] = 1.0
    h_ltc = bf(np.random.standard_normal((B, HID)))
    x_t = bf(np.random.standard_normal((B, IN_DIM)) * s[:IN_DIM])
    context = bf(np.random.standard_normal((B, ATT)) * s[IN_DIM + HID:])
    w_gd = np.random.uniform(-1.0, 1.0, (2 * HID, TOTAL)) * 3.0 / np.sqrt(TOTAL) / s[None, :]
    W_gd_words, W_gd_scales = pack_weight(np.ascontiguousarray(w_gd.T), "e4m3")
    return {"t": 0.0,
            "h_ltc": h_ltc,
            "x_t": x_t,
            "context": context,
            "W_gd_words": W_gd_words,
            "W_gd_scales": W_gd_scales,
            "b_gd": bf(np.random.uniform(-0.1, 0.1, (2 * HID,))),
            "W_tau": bf(np.random.uniform(-1.0, 1.0, (HID, HID)) * 2.0 / np.sqrt(HID)),
            "b_tau": bf(np.random.uniform(-0.1, 0.1, (HID,))),
            "gleak": bf(np.random.uniform(0.001, 1.0, (HID,))),
            "cm": bf(np.random.uniform(0.4, 0.6, (HID,)))}


def reference(t, h_ltc, x_t, context, W_gd_words, W_gd_scales, b_gd, W_tau, b_tau, gleak, cm):
    h = f64(h_ltc)
    combined = np.concatenate([f64(x_t), h, f64(context)], axis=1)
    g_d = (mxq(combined, 1, "e4m3") @ unpack_weight(W_gd_words, W_gd_scales, "e4m3")) + f64(b_gd)
    gate, dynamics = np.split(g_d, 2, axis=1)
    tau = softplus(h @ f64(W_tau).T + f64(b_tau))
    numerator = sigmoid(gate) * np.tanh(dynamics) - h
    denominator = tau + softplus(f64(cm)) + softplus(f64(gleak))
    return numerator / (denominator + 1e-6)

@@ -1,0 +1,376 @@
+from contextlib import ExitStack
+
+import concourse.mybir as mybir
+from concourse.masks import make_identity
+
+F32 = mybir.dt.float32
+BF16 = mybir.dt.bfloat16
+U32 = mybir.dt.uint32
+U8 = mybir.dt.uint8
+I32 = mybir.dt.int32
+FP8X4 = mybir.dt.float8_e4m3fn_x4
+ALU = mybir.AluOpType
+ACT = mybir.ActivationFunctionType
+
+P = 128
+FLOPS = 2 * 128 * 4096 * 4096 + 2 * 128 * 2048 * 2048
+
+PINNED = True
+SEGS = [(0, 512), (512, 512), (1024, 512), (1536, 512)]
+SEG_TAG = ["B", "B", "A", "A"]
+TILES = [
+    [(0, 0, 1024), (1, 0, 1024)],
+    [(2, 0, 1024), (3, 0, 1024)],
+    [(4, 0, 1024), (5, 0, 1024)],
+    [(6, 0, 1024), (7, 0, 1024)],
+    [(0, 1024, 1024), (1, 1024, 1024)],
+    [(2, 1024, 1024), (3, 1024, 1024)],
+    [(4, 1024, 512), (5, 1024, 512), (6, 1024, 512), (7, 1024, 512)],
+    [(4, 1536, 512), (5, 1536, 512), (6, 1536, 512), (7, 1536, 512)],
+]
+
+
+def tile_ltcattentioncell_w_kernel(
+    tc, t, h_ltc, x_t, context, W_gd_words, W_gd_scales, b_gd, W_tau, b_tau, gleak, cm, out
+):
+    nc = tc.nc
+    with ExitStack() as ctx:
+        const = ctx.enter_context(tc.tile_pool(name="const", bufs=1))
+        big = ctx.enter_context(tc.tile_pool(name="big", bufs=7))
+        wtp = ctx.enter_context(tc.tile_pool(name="wtp", bufs=6))
+        ep = ctx.enter_context(tc.tile_pool(name="ep", bufs=3))
+        ps_a = ctx.enter_context(tc.psum_pool(name="psa", bufs=4))
+        ps_b = ctx.enter_context(tc.psum_pool(name="psb", bufs=4))
+        if PINNED:
+            ctx.enter_context(tc.manual_schedule())
+
+        ident_f = const.tile([P, P], F32)
+        ident_b = const.tile([P, P], BF16)
+        rows = const.tile([P, P], BF16)
+        planes = const.tile([P, 2, 4096], U8, align_bytes=64)
+        comb = const.tile([P, 4096], BF16, align_bytes=64)
+        grouped = const.tile([P, 4096], BF16, align_bytes=64)
+        codes = const.tile([P, 1024], U32, align_bytes=64)
+        ascl = const.tile([P, 1024], U8, align_bytes=64)
+        h_t = const.tile([P, 8, 2, P], BF16)
+        bgd_b = const.tile([P, 4096], BF16)
+        c_b = const.tile([P, 2048], F32)
+        el = const.tile([P, 2048], F32)
+        rr = const.tile([P, 2048], F32)
+        stb = const.tile([P, 32], BF16)
+        gc = const.tile([P, 32], F32)
+        gl = const.tile([P, 32], F32)
+        sp = const.tile([P, 32], F32)
+        c_t = const.tile([P, 16], F32)
+
+        nc.vector.memset(rows[:], 0.0)
+        nc.vector.memset(planes[:].rearrange("p a n -> p (a n)").bitcast(I32), 0)
+        make_identity(nc, ident_f[:])
+        make_identity(nc, ident_b[:])
+
+        nc.sync.dma_start(out=comb[:, 512:2560], in_=h_ltc)
+        nc.scalar.dma_start(out=rows[0:32, :], in_=b_gd.rearrange("(r c) -> r c", c=P))
+        nc.scalar.dma_start(out=rows[32:48, :], in_=b_tau.rearrange("(r c) -> r c", c=P))
+        nc.scalar.dma_start(out=rows[48:64, :], in_=gleak.rearrange("(r c) -> r c", c=P))
+        nc.scalar.dma_start(out=rows[64:80, :], in_=cm.rearrange("(r c) -> r c", c=P))
+        nc.sync.dma_start(out=comb[:, 0:512], in_=x_t)
+        nc.sync.dma_start(out=comb[:, 2560:4096], in_=context)
+        wraw = []
+        for d in range(4):
+            wr = big.tile([P, 4, 2048], BF16, tag="big", name="wraw%d" % d, align_bytes=64)
+            nc.sync.dma_start(
+                out=wr[:], in_=W_tau[512 * d : 512 * d + 512, :].rearrange("(p t) i -> p t i", t=4)
+            )
+            wraw.append(wr)
+        for a in range(2):
+            for q in (0, 2, 1, 3):
+                nc.sync.dma_start(
+                    out=planes[32 * q : 32 * q + 16, a, :].bitcast(I32),
+                    in_=W_gd_scales[4 * a : 4 * a + 4, 4 * q : 4 * q + 4, :].bitcast(I32),
+                )
+
+        wtiles = {}
+
+        def issue_tile(k):
+            wt = big.tile([P, 4096], U32, tag="big", name="wgd%d" % k, align_bytes=64)
+            off = 0
+            for g, o0, width in TILES[k]:
+                src = (
+                    W_gd_words[g]
+                    .rearrange("p n t -> p (n t)")
+                    .rearrange("p (s m) -> p s m", s=2)[:, :, 4 * o0 : 4 * (o0 + width)]
+                    .bitcast(I32)
+                )
+                dst = wt[:, off : off + 2 * width].rearrange("p (s m) -> p s m", s=2).bitcast(I32)
+                nc.sync.dma_start(out=dst, in_=src)
+                off += 2 * width
+            wtiles[k] = wt
+
+        for k in range(3):
+            issue_tile(k)
+
+        combw = comb[:].bitcast(F32)
+        for k in range(2):
+            hps = ps_a.tile([P, 4, P], F32, tag="A", name="hps%d" % k)
+            for cc in range(4):
+                c = 4 * k + cc
+                nc.tensor.transpose(
+                    out=hps[:, cc, :], in_=combw[:, 256 + P * c : 256 + P * c + P], identity=ident_f[:]
+                )
+            src = hps[:].bitcast(BF16).rearrange("q c (b e) -> q c e b", e=2)
+            if k == 0:
+                nc.vector.tensor_copy(out=h_t[:, 0:4, :, :], in_=src)
+            else:
+                nc.scalar.copy(out=h_t[:, 4:8, :, :], in_=src)
+
+        gview = grouped[:].bitcast(F32).rearrange("p (g b u) -> p g b u", g=8, u=2)
+        for k in range(4):
+            xg = ps_a.tile([P, 2, 2, P], F32, tag="A", name="xg%d" % k)
+            for gi in range(2):
+                g = 2 * k + gi
+                for u in range(2):
+                    nc.tensor.transpose(
+                        out=xg[:, gi, u, :],
+                        in_=combw[:, 256 * g + u : 256 * (g + 1) : 2],
+                        identity=ident_f[:],
+                    )
+            src = xg[:].rearrange("p g u b -> p g b u")
+            if k % 2 == 0:
+                nc.vector.tensor_copy(out=gview[:, 2 * k : 2 * k + 2], in_=src)
+            else:
+                nc.scalar.copy(out=gview[:, 2 * k : 2 * k + 2], in_=src)
+
+        st_ps = ps_a.tile([P, P], BF16, tag="A", name="st_ps")
+        nc.tensor.transpose(out=st_ps[:], in_=rows[:], identity=ident_b[:])
+        nc.vector.tensor_copy(out=gc[:], in_=st_ps[:, 48:80])
+        nc.vector.tensor_copy(out=stb[:], in_=st_ps[:, 0:32])
+        nc.scalar.activation(out=gl[:], in_=gc[:], func=ACT.Abs)
+        nc.scalar.activation(out=gl[:], in_=gl[:], func=ACT.Exp, scale=-1.0)
+        nc.scalar.activation(out=gl[:], in_=gl[:], func=ACT.Ln, bias=1.0)
+        for half in range(2):
+            nc.vector.quantize_mx(
+                out=codes[:, 512 * half : 512 * half + 512].bitcast(FP8X4),
+                scales=ascl[:, 512 * half : 512 * half + 512],
+                in_=grouped[:, 2048 * half : 2048 * half + 2048],
+            )
+        nc.vector.scalar_tensor_tensor(
+            out=sp[:], in0=gc[:], scalar=0.0, in1=gl[:], op0=ALU.max, op1=ALU.add
+        )
+        nc.vector.scalar_tensor_tensor(
+            out=c_t[:], in0=sp[:, 0:16], scalar=1e-6, in1=sp[:, 16:32], op0=ALU.add, op1=ALU.add
+        )
+
+        def broadcast_c():
+            for k in range(4):
+                cps = ps_a.tile([P, 4, P], F32, tag="A", name="cps%d" % k)
+                for jj in range(4):
+                    col = 4 * k + jj
+                    nc.tensor.transpose(
+                        out=cps[:, jj, :],
+                        in_=c_t[:, col : col + 1].to_broadcast([P, P]),
+                        identity=ident_f[:],
+                    )
+                src = cps[:].rearrange("p j n -> p (j n)")
+                if k % 2 == 0:
+                    nc.vector.tensor_copy(out=c_b[:, 512 * k : 512 * k + 512], in_=src)
+                else:
+                    nc.scalar.copy(out=c_b[:, 512 * k : 512 * k + 512], in_=src)
+
+        def broadcast_bgd():
+            for k in range(4):
+                bps = ps_a.tile([P, 8, P], BF16, tag="A", name="bps%d" % k)
+                for jj in range(8):
+                    col = 8 * k + jj
+                    nc.tensor.transpose(
+                        out=bps[:, jj, :],
+                        in_=stb[:, col : col + 1].to_broadcast([P, P]),
+                        identity=ident_b[:],
+                    )
+                src = bps[:].rearrange("p j n -> p (j n)")
+                if k % 2 == 0:
+                    nc.vector.tensor_copy(out=bgd_b[:, 1024 * k : 1024 * k + 1024], in_=src)
+                else:
+                    nc.scalar.copy(out=bgd_b[:, 1024 * k : 1024 * k + 1024], in_=src)
+
+        tps = {}
+        wts = {}
+        tau_ps = []
+
+        def unit_transposes(u, which):
+            d, c = divmod(u, 8)
+            if u not in tps:
+                tps[u] = ps_a.tile([P, 4, P], F32, tag="A", name="tp%d" % u)
+            words = wraw[d][:].bitcast(F32)
+            for tt in which:
+                nc.tensor.transpose(
+                    out=tps[u][:, tt, :], in_=words[:, tt, P * c : P * c + P], identity=ident_f[:]
+                )
+
+        def unit_copy(u):
+            wt = wtp.tile([P, 512], F32, tag="wt", name="wt%d" % u)
+            dst = wt[:].rearrange("q (p t) -> q p t", t=4)
+            src = tps[u][:].rearrange("q t p -> q p t")
+            if u % 2 == 0:
+                nc.scalar.copy(out=dst, in_=src)
+            else:
+                nc.vector.tensor_copy(out=dst, in_=src)
+            wts[u] = wt
+
+        def unit_matmul(u, e):
+            d, c = divmod(u, 8)
+            if c == 0 and e == 0:
+                tau_ps.append(ps_b.tile([P, 512], F32, tag="B", name="tau%d" % d))
+            rhs = wts[u][:].bitcast(BF16).rearrange("q (o e) -> q o e", e=2)[:, :, e]
+            nc.tensor.matmul(
+                out=tau_ps[d][:],
+                lhsT=h_t[:, c, e, :],
+                rhs=rhs,
+                start=(c == 0 and e == 0),
+                stop=(c == 7 and e == 1),
+            )
+
+        def tau_bias(d):
+            for jj in range(4):
+                r = 32 + 4 * d + jj
+                nc.tensor.matmul(
+                    out=tau_ps[d][:, P * jj : P * jj + P],
+                    lhsT=ident_b[:, r : r + 1].to_broadcast([P, P]),
+                    rhs=rows[:],
+                    start=False,
+                    stop=False,
+                )
+
+        def tau_part1(d):
+            blk = slice(512 * d, 512 * d + 512)
+            nc.scalar.activation(out=el[:, blk], in_=tau_ps[d][:], func=ACT.Abs)
+            nc.vector.scalar_tensor_tensor(
+                out=rr[:, blk], in0=tau_ps[d][:], scalar=0.0, in1=c_b[:, blk], op0=ALU.max, op1=ALU.add
+            )
+            nc.scalar.activation(out=el[:, blk], in_=el[:, blk], func=ACT.Exp, scale=-1.0)
+
+        AHEAD = 3
+        for u in range(AHEAD):
+            unit_transposes(u, (0, 1, 2, 3))
+            unit_copy(u)
+        broadcast_c()
+        for u in range(32):
+            nxt = u + AHEAD
+            if nxt < 32:
+                unit_transposes(nxt, (0, 1))
+            unit_matmul(u, 0)
+            if nxt < 32:
+                unit_transposes(nxt, (2, 3))
+            unit_matmul(u, 1)
+            if u % 8 == 2:
+                tau_bias(u // 8)
+            if nxt < 32:
+                unit_copy(nxt)
+            if u % 8 == 4:
+                issue_tile(3 + u // 8)
+            if u >= 9 and (u - 9) % 8 == 0:
+                tau_part1((u - 9) // 8)
+        tau_part1(3)
+        broadcast_bgd()
+
+        blks = [slice(512 * d, 512 * d + 512) for d in range(4)]
+        for blk in blks:
+            nc.scalar.activation(out=el[:, blk], in_=el[:, blk], func=ACT.Ln, bias=1.0)
+            nc.vector.tensor_tensor(out=rr[:, blk], in0=rr[:, blk], in1=el[:, blk], op=ALU.add)
+        for blk in blks:
+            nc.scalar.activation(out=rr[:, blk], in_=rr[:, blk], func=ACT.Ln, scale=2.0)
+        for d in range(4):
+            blk = blks[d]
+            nc.scalar.activation(out=rr[:, blk], in_=rr[:, blk], func=ACT.Exp, scale=-1.0)
+            nc.vector.scalar_tensor_tensor(
+                out=el[:, blk],
+                in0=comb[:, 512 + 512 * d : 1024 + 512 * d],
+                scalar=2.0,
+                in1=rr[:, blk],
+                op0=ALU.mult,
+                op1=ALU.mult,
+            )
+
+        banks = {}
+        done = {}
+        temps = {}
+
+        def consume_tile(k):
+            off = 0
+            for g, o0, width in TILES[k]:
+                for si in range(len(SEGS)):
+                    s0, sw = SEGS[si]
+                    if s0 < o0 or s0 + sw > o0 + width:
+                        continue
+                    if si not in banks:
+                        pool = ps_a if SEG_TAG[si] == "A" else ps_b
+                        dps = pool.tile([P, 512], F32, tag=SEG_TAG[si], name="dps%d" % si)
+                        gps = pool.tile([P, 512], F32, tag=SEG_TAG[si], name="gps%d" % si)
+                        banks[si] = (gps, dps)
+                    for half in (1, 0):
+                        n_done = done.get((si, half), 0)
+                        w0 = off + half * width + (s0 - o0)
+                        n0 = 2048 * half + s0
+                        kk = 4 * (g % 4)
+                        nc.tensor.matmul_mx(
+                            out=banks[si][half][:, 0:sw],
+                            lhsT=codes[:, P * g : P * g + P].bitcast(FP8X4),
+                            lhsT_scale=ascl[:, P * g : P * g + P],
+                            rhs=wtiles[k][:, w0 : w0 + sw].bitcast(FP8X4),
+                            rhs_scale=planes[kk:P, g // 4, n0 : n0 + sw],
+                            start=(n_done == 0),
+                            stop=(n_done == 7),
+                        )
+                        done[(si, half)] = n_done + 1
+                off += 2 * width
+
+        def epilogue1(si):
+            s0, sw = SEGS[si]
+            gps, dps = banks[si]
+            da = ep.tile([P, 512], F32, tag="da", name="da%d" % si)
+            ga = ep.tile([P, 512], F32, tag="ga", name="ga%d" % si)
+            nc.vector.tensor_tensor(
+                out=da[:, 0:sw], in0=dps[:, 0:sw], in1=bgd_b[:, 2048 + s0 : 2048 + s0 + sw], op=ALU.add
+            )
+            nc.scalar.activation(out=da[:, 0:sw], in_=da[:, 0:sw], func=ACT.Tanh)
+            nc.vector.tensor_tensor(
+                out=ga[:, 0:sw], in0=gps[:, 0:sw], in1=bgd_b[:, s0 : s0 + sw], op=ALU.add
+            )
+            nc.scalar.activation(out=ga[:, 0:sw], in_=ga[:, 0:sw], func=ACT.Tanh, scale=0.5)
+            temps[si] = (ga, da)
+
+        def epilogue2(si):
+            s0, sw = SEGS[si]
+            ga, da = temps[si]
+            ot = ep.tile([P, 512], F32, tag="ot", name="ot%d" % si)
+            nc.vector.tensor_tensor(
+                out=da[:, 0:sw], in0=da[:, 0:sw], in1=rr[:, s0 : s0 + sw], op=ALU.mult
+            )
+            nc.vector.scalar_tensor_tensor(
+                out=ga[:, 0:sw], in0=ga[:, 0:sw], scalar=1.0, in1=da[:, 0:sw], op0=ALU.add, op1=ALU.mult
+            )
+            nc.vector.tensor_tensor(
+                out=ot[:, 0:sw], in0=ga[:, 0:sw], in1=el[:, s0 : s0 + sw], op=ALU.subtract
+            )
+            return ot
+
+        consume_tile(0)
+        issue_tile(7)
+        consume_tile(1)
+        consume_tile(2)
+        consume_tile(3)
+        epilogue1(0)
+        epilogue1(1)
+        for si in (0, 1):
+            s0, sw = SEGS[si]
+            ot = epilogue2(si)
+            nc.scalar.dma_start(out=out[:, s0 : s0 + sw], in_=ot[:, 0:sw])
+        consume_tile(4)
+        consume_tile(5)
+        consume_tile(6)
+        for si in (2, 3):
+            if si == 3:
+                consume_tile(7)
+            s0, sw = SEGS[si]
+            epilogue1(si)
+            ot = epilogue2(si)
+            nc.sync.dma_start(out=out[:, s0 : s0 + sw], in_=ot[:, 0:sw])

@@ -67,6 +67,12 @@ def tile_ltcattentioncell_w_kernel(
         nc.vector.memset(planes[:].rearrange("p a n -> p (a n)").bitcast(I32), 0)
         make_identity(nc, ident_f[:])
         make_identity(nc, ident_b[:])
+        for a in range(2):
+            for q in (0, 2, 1, 3):
+                nc.gpsimd.dma_start(
+                    out=planes[32 * q : 32 * q + 16, a, :].bitcast(F32),
+                    in_=W_gd_scales[4 * a : 4 * a + 4, 4 * q : 4 * q + 4, :].bitcast(F32),
+                )
 
         nc.sync.dma_start(out=comb[:, 512:2560], in_=h_ltc)
         nc.scalar.dma_start(out=rows[0:32, :], in_=b_gd.rearrange("(r c) -> r c", c=P))
@@ -82,12 +88,6 @@ def tile_ltcattentioncell_w_kernel(
                 out=wr[:], in_=W_tau[512 * d : 512 * d + 512, :].rearrange("(p t) i -> p t i", t=4)
             )
             wraw.append(wr)
-        for a in range(2):
-            for q in (0, 2, 1, 3):
-                nc.sync.dma_start(
-                    out=planes[32 * q : 32 * q + 16, a, :].bitcast(I32),
-                    in_=W_gd_scales[4 * a : 4 * a + 4, 4 * q : 4 * q + 4, :].bitcast(I32),
-                )
 
         wtiles = {}
 

@@ -16,17 +16,24 @@ P = 128
 FLOPS = 2 * 128 * 4096 * 4096 + 2 * 128 * 2048 * 2048
 
 PINNED = True
-SEGS = [(0, 512), (512, 512), (1024, 512), (1536, 512)]
-SEG_TAG = ["B", "B", "A", "A"]
+SEGS = [(0, 512), (512, 512), (1024, 512), (1536, 256), (1792, 256)]
+SEG_TAG = ["B", "B", "A", "A", "B"]
+BOTH = (1, 0)
 TILES = [
-    [(0, 0, 1024), (1, 0, 1024)],
-    [(2, 0, 1024), (3, 0, 1024)],
-    [(4, 0, 1024), (5, 0, 1024)],
-    [(6, 0, 1024), (7, 0, 1024)],
-    [(0, 1024, 1024), (1, 1024, 1024)],
-    [(2, 1024, 1024), (3, 1024, 1024)],
-    [(4, 1024, 512), (5, 1024, 512), (6, 1024, 512), (7, 1024, 512)],
-    [(4, 1536, 512), (5, 1536, 512), (6, 1536, 512), (7, 1536, 512)],
+    [((0,), BOTH, 0, 1024), ((1,), BOTH, 0, 1024)],
+    [((2,), BOTH, 0, 1024), ((3,), BOTH, 0, 1024)],
+    [((4,), BOTH, 0, 1024), ((5,), BOTH, 0, 1024)],
+    [((6,), BOTH, 0, 1024), ((7,), BOTH, 0, 1024)],
+    [((0,), BOTH, 1024, 1024), ((1,), BOTH, 1024, 1024)],
+    [((2,), BOTH, 1024, 1024), ((3,), BOTH, 1024, 1024)],
+    [((4,), BOTH, 1024, 512), ((5,), BOTH, 1024, 512), ((6,), BOTH, 1024, 512), ((7,), BOTH, 1024, 512)],
+    [
+        ((4,), BOTH, 1536, 512),
+        ((5,), BOTH, 1536, 512),
+        ((6, 7), (1,), 1536, 512),
+        ((6, 7), (0,), 1536, 256),
+        ((6, 7), (0,), 1792, 256),
+    ],
 ]
 
 
@@ -67,40 +74,52 @@ def tile_ltcattentioncell_w_kernel(
         nc.vector.memset(planes[:].rearrange("p a n -> p (a n)").bitcast(I32), 0)
         make_identity(nc, ident_f[:])
         make_identity(nc, ident_b[:])
-        for a in range(2):
-            for q in (0, 2, 1, 3):
-                nc.gpsimd.dma_start(
-                    out=planes[32 * q : 32 * q + 16, a, :].bitcast(F32),
-                    in_=W_gd_scales[4 * a : 4 * a + 4, 4 * q : 4 * q + 4, :].bitcast(F32),
-                )
 
         nc.sync.dma_start(out=comb[:, 512:2560], in_=h_ltc)
         nc.scalar.dma_start(out=rows[0:32, :], in_=b_gd.rearrange("(r c) -> r c", c=P))
         nc.scalar.dma_start(out=rows[32:48, :], in_=b_tau.rearrange("(r c) -> r c", c=P))
         nc.scalar.dma_start(out=rows[48:64, :], in_=gleak.rearrange("(r c) -> r c", c=P))
         nc.scalar.dma_start(out=rows[64:80, :], in_=cm.rearrange("(r c) -> r c", c=P))
-        nc.sync.dma_start(out=comb[:, 0:512], in_=x_t)
-        nc.sync.dma_start(out=comb[:, 2560:4096], in_=context)
         wraw = []
         for d in range(4):
             wr = big.tile([P, 4, 2048], BF16, tag="big", name="wraw%d" % d, align_bytes=64)
-            nc.sync.dma_start(
-                out=wr[:], in_=W_tau[512 * d : 512 * d + 512, :].rearrange("(p t) i -> p t i", t=4)
-            )
+            w_src = W_tau[512 * d : 512 * d + 512, :].rearrange("(p t) i -> p t i", t=4)
+            if d == 0:
+                nc.sync.dma_start(out=wr[:, :, 0:1024], in_=w_src[:, :, 0:1024])
+                nc.sync.dma_start(out=wr[:, :, 1024:2048], in_=w_src[:, :, 1024:2048])
+            else:
+                nc.sync.dma_start(out=wr[:], in_=w_src)
             wraw.append(wr)
+            if d == 1:
+                nc.sync.dma_start(out=comb[:, 0:512], in_=x_t)
+                nc.sync.dma_start(out=comb[:, 2560:4096], in_=context)
+        for a in range(2):
+            for q in (0, 2, 1, 3):
+                nc.sync.dma_start(
+                    out=planes[32 * q : 32 * q + 16, a, :].bitcast(I32),
+                    in_=W_gd_scales[4 * a : 4 * a + 4, 4 * q : 4 * q + 4, :].bitcast(I32),
+                )
 
         wtiles = {}
 
         def issue_tile(k):
             wt = big.tile([P, 4096], U32, tag="big", name="wgd%d" % k, align_bytes=64)
             off = 0
-            for g, o0, width in TILES[k]:
-                src = (
-                    W_gd_words[g]
-                    .rearrange("p n t -> p (n t)")
-                    .rearrange("p (s m) -> p s m", s=2)[:, :, 4 * o0 : 4 * (o0 + width)]
-                    .bitcast(I32)
-                )
+            for gs, halves, o0, width in TILES[k]:
+                if len(halves) == 2:
+                    src = (
+                        W_gd_words[gs[0]]
+                        .rearrange("p n t -> p (n t)")
+                        .rearrange("p (s m) -> p s m", s=2)[:, :, 4 * o0 : 4 * (o0 + width)]
+                        .bitcast(I32)
+                    )
+                else:
+                    n0 = 2048 * halves[0] + o0
+                    src = (
+                        W_gd_words[gs[0] : gs[0] + len(gs)]
+                        .rearrange("g p n t -> p g (n t)")[:, :, 4 * n0 : 4 * (n0 + width)]
+                        .bitcast(I32)
+                    )
                 dst = wt[:, off : off + 2 * width].rearrange("p (s m) -> p s m", s=2).bitcast(I32)
                 nc.sync.dma_start(out=dst, in_=src)
                 off += 2 * width
@@ -124,21 +143,31 @@ def tile_ltcattentioncell_w_kernel(
                 nc.scalar.copy(out=h_t[:, 4:8, :, :], in_=src)
 
         gview = grouped[:].bitcast(F32).rearrange("p (g b u) -> p g b u", g=8, u=2)
-        for k in range(4):
-            xg = ps_a.tile([P, 2, 2, P], F32, tag="A", name="xg%d" % k)
-            for gi in range(2):
-                g = 2 * k + gi
-                for u in range(2):
-                    nc.tensor.transpose(
-                        out=xg[:, gi, u, :],
-                        in_=combw[:, 256 * g + u : 256 * (g + 1) : 2],
-                        identity=ident_f[:],
-                    )
-            src = xg[:].rearrange("p g u b -> p g b u")
-            if k % 2 == 0:
-                nc.vector.tensor_copy(out=gview[:, 2 * k : 2 * k + 2], in_=src)
-            else:
-                nc.scalar.copy(out=gview[:, 2 * k : 2 * k + 2], in_=src)
+
+        def transpose_combined():
+            for k in range(4):
+                xg = ps_a.tile([P, 2, 2, P], F32, tag="A", name="xg%d" % k)
+                for gi in range(2):
+                    g = 2 * k + gi
+                    for u in range(2):
+                        nc.tensor.transpose(
+                            out=xg[:, gi, u, :],
+                            in_=combw[:, 256 * g + u : 256 * (g + 1) : 2],
+                            identity=ident_f[:],
+                        )
+                src = xg[:].rearrange("p g u b -> p g b u")
+                if k % 2 == 0:
+                    nc.vector.tensor_copy(out=gview[:, 2 * k : 2 * k + 2], in_=src)
+                else:
+                    nc.scalar.copy(out=gview[:, 2 * k : 2 * k + 2], in_=src)
+
+        def quantise_combined():
+            for half in range(2):
+                nc.vector.quantize_mx(
+                    out=codes[:, 512 * half : 512 * half + 512].bitcast(FP8X4),
+                    scales=ascl[:, 512 * half : 512 * half + 512],
+                    in_=grouped[:, 2048 * half : 2048 * half + 2048],
+                )
 
         st_ps = ps_a.tile([P, P], BF16, tag="A", name="st_ps")
         nc.tensor.transpose(out=st_ps[:], in_=rows[:], identity=ident_b[:])
@@ -147,12 +176,6 @@ def tile_ltcattentioncell_w_kernel(
         nc.scalar.activation(out=gl[:], in_=gc[:], func=ACT.Abs)
         nc.scalar.activation(out=gl[:], in_=gl[:], func=ACT.Exp, scale=-1.0)
         nc.scalar.activation(out=gl[:], in_=gl[:], func=ACT.Ln, bias=1.0)
-        for half in range(2):
-            nc.vector.quantize_mx(
-                out=codes[:, 512 * half : 512 * half + 512].bitcast(FP8X4),
-                scales=ascl[:, 512 * half : 512 * half + 512],
-                in_=grouped[:, 2048 * half : 2048 * half + 2048],
-            )
         nc.vector.scalar_tensor_tensor(
             out=sp[:], in0=gc[:], scalar=0.0, in1=gl[:], op0=ALU.max, op1=ALU.add
         )
@@ -210,7 +233,7 @@ def tile_ltcattentioncell_w_kernel(
             wt = wtp.tile([P, 512], F32, tag="wt", name="wt%d" % u)
             dst = wt[:].rearrange("q (p t) -> q p t", t=4)
             src = tps[u][:].rearrange("q t p -> q p t")
-            if u % 2 == 0:
+            if u % 2 == 0 and u >= 8:
                 nc.scalar.copy(out=dst, in_=src)
             else:
                 nc.vector.tensor_copy(out=dst, in_=src)
@@ -252,7 +275,6 @@ def tile_ltcattentioncell_w_kernel(
         for u in range(AHEAD):
             unit_transposes(u, (0, 1, 2, 3))
             unit_copy(u)
-        broadcast_c()
         for u in range(32):
             nxt = u + AHEAD
             if nxt < 32:
@@ -267,6 +289,12 @@ def tile_ltcattentioncell_w_kernel(
                 unit_copy(nxt)
             if u % 8 == 4:
                 issue_tile(3 + u // 8)
+            if u == 6:
+                broadcast_c()
+            if u == 14:
+                transpose_combined()
+            if u == 17:
+                quantise_combined()
             if u >= 9 and (u - 9) % 8 == 0:
                 tau_part1((u - 9) // 8)
         tau_part1(3)
@@ -294,9 +322,11 @@ def tile_ltcattentioncell_w_kernel(
         done = {}
         temps = {}
 
-        def consume_tile(k):
-            off = 0
-            for g, o0, width in TILES[k]:
+        def consume_dma(k, j):
+            off = sum([2 * e[3] for e in TILES[k][:j]])
+            gs, halves, o0, width = TILES[k][j]
+            for gi in range(len(gs)):
+                g = gs[gi]
                 for si in range(len(SEGS)):
                     s0, sw = SEGS[si]
                     if s0 < o0 or s0 + sw > o0 + width:
@@ -306,9 +336,10 @@ def tile_ltcattentioncell_w_kernel(
                         dps = pool.tile([P, 512], F32, tag=SEG_TAG[si], name="dps%d" % si)
                         gps = pool.tile([P, 512], F32, tag=SEG_TAG[si], name="gps%d" % si)
                         banks[si] = (gps, dps)
-                    for half in (1, 0):
+                    for half in halves:
                         n_done = done.get((si, half), 0)
-                        w0 = off + half * width + (s0 - o0)
+                        row = half if len(halves) == 2 else gi
+                        w0 = off + row * width + (s0 - o0)
                         n0 = 2048 * half + s0
                         kk = 4 * (g % 4)
                         nc.tensor.matmul_mx(
@@ -321,56 +352,73 @@ def tile_ltcattentioncell_w_kernel(
                             stop=(n_done == 7),
                         )
                         done[(si, half)] = n_done + 1
-                off += 2 * width
 
-        def epilogue1(si):
-            s0, sw = SEGS[si]
-            gps, dps = banks[si]
-            da = ep.tile([P, 512], F32, tag="da", name="da%d" % si)
-            ga = ep.tile([P, 512], F32, tag="ga", name="ga%d" % si)
-            nc.vector.tensor_tensor(
-                out=da[:, 0:sw], in0=dps[:, 0:sw], in1=bgd_b[:, 2048 + s0 : 2048 + s0 + sw], op=ALU.add
-            )
-            nc.scalar.activation(out=da[:, 0:sw], in_=da[:, 0:sw], func=ACT.Tanh)
-            nc.vector.tensor_tensor(
-                out=ga[:, 0:sw], in0=gps[:, 0:sw], in1=bgd_b[:, s0 : s0 + sw], op=ALU.add
-            )
-            nc.scalar.activation(out=ga[:, 0:sw], in_=ga[:, 0:sw], func=ACT.Tanh, scale=0.5)
-            temps[si] = (ga, da)
+        def consume_tile(k):
+            for j in range(len(TILES[k])):
+                consume_dma(k, j)
 
-        def epilogue2(si):
+        def ep_add(si, half):
             s0, sw = SEGS[si]
-            ga, da = temps[si]
-            ot = ep.tile([P, 512], F32, tag="ot", name="ot%d" % si)
+            tmp = ep.tile([P, 512], F32, tag="add%d" % half, name="add%d_%d" % (half, si))
+            nc.vector.tensor_tensor(
+                out=tmp[:, 0:sw],
+                in0=banks[si][half][:, 0:sw],
+                in1=bgd_b[:, 2048 * half + s0 : 2048 * half + s0 + sw],
+                op=ALU.add,
+            )
+            nc.scalar.activation(
+                out=tmp[:, 0:sw], in_=tmp[:, 0:sw], func=ACT.Tanh, scale=(1.0 if half == 1 else 0.5)
+            )
+            temps[(si, half)] = tmp
+
+        def ep_w(si):
+            s0, sw = SEGS[si]
+            da = temps[(si, 1)]
             nc.vector.tensor_tensor(
                 out=da[:, 0:sw], in0=da[:, 0:sw], in1=rr[:, s0 : s0 + sw], op=ALU.mult
             )
+
+        def ep_out(si, queue):
+            s0, sw = SEGS[si]
+            da = temps[(si, 1)]
+            ga = temps[(si, 0)]
+            ot = ep.tile([P, 512], F32, tag="ot", name="ot%d" % si)
             nc.vector.scalar_tensor_tensor(
                 out=ga[:, 0:sw], in0=ga[:, 0:sw], scalar=1.0, in1=da[:, 0:sw], op0=ALU.add, op1=ALU.mult
             )
             nc.vector.tensor_tensor(
                 out=ot[:, 0:sw], in0=ga[:, 0:sw], in1=el[:, s0 : s0 + sw], op=ALU.subtract
             )
-            return ot
+            queue.dma_start(out=out[:, s0 : s0 + sw], in_=ot[:, 0:sw])
 
         consume_tile(0)
         issue_tile(7)
         consume_tile(1)
         consume_tile(2)
         consume_tile(3)
-        epilogue1(0)
-        epilogue1(1)
         for si in (0, 1):
-            s0, sw = SEGS[si]
-            ot = epilogue2(si)
-            nc.scalar.dma_start(out=out[:, s0 : s0 + sw], in_=ot[:, 0:sw])
+            ep_add(si, 1)
+            ep_add(si, 0)
+        for si in (0, 1):
+            ep_w(si)
+            ep_out(si, nc.scalar)
         consume_tile(4)
         consume_tile(5)
         consume_tile(6)
-        for si in (2, 3):
-            if si == 3:
-                consume_tile(7)
-            s0, sw = SEGS[si]
-            epilogue1(si)
-            ot = epilogue2(si)
-            nc.sync.dma_start(out=out[:, s0 : s0 + sw], in_=ot[:, 0:sw])
+        ep_add(2, 1)
+        ep_add(2, 0)
+        ep_w(2)
+        ep_out(2, nc.sync)
+        consume_dma(7, 0)
+        consume_dma(7, 1)
+        consume_dma(7, 2)
+        ep_add(3, 1)
+        ep_add(4, 1)
+        ep_w(3)
+        ep_w(4)
+        consume_dma(7, 3)
+        ep_add(3, 0)
+        ep_out(3, nc.sync)
+        consume_dma(7, 4)
+        ep_add(4, 0)
+        ep_out(4, nc.sync)

@@ -16,9 +16,18 @@ P = 128
 FLOPS = 2 * 128 * 4096 * 4096 + 2 * 128 * 2048 * 2048
 
 PINNED = True
-SEGS = [(0, 512), (512, 512), (1024, 512), (1536, 256), (1792, 256)]
-SEG_TAG = ["B", "B", "A", "A", "B"]
 BOTH = (1, 0)
+GROUPS = [
+    (1, 0, 512, "B"),
+    (0, 0, 512, "B"),
+    (1, 512, 512, "B"),
+    (0, 512, 512, "B"),
+    (1, 1024, 512, "A"),
+    (0, 1024, 512, "A"),
+    (1, 1536, 512, "A"),
+    (0, 1536, 256, "A"),
+    (0, 1792, 256, "B"),
+]
 TILES = [
     [((0,), BOTH, 0, 1024), ((1,), BOTH, 0, 1024)],
     [((2,), BOTH, 0, 1024), ((3,), BOTH, 0, 1024)],
@@ -28,9 +37,9 @@ TILES = [
     [((2,), BOTH, 1024, 1024), ((3,), BOTH, 1024, 1024)],
     [((4,), BOTH, 1024, 512), ((5,), BOTH, 1024, 512), ((6,), BOTH, 1024, 512), ((7,), BOTH, 1024, 512)],
     [
-        ((4,), BOTH, 1536, 512),
-        ((5,), BOTH, 1536, 512),
+        ((4, 5), (1,), 1536, 512),
         ((6, 7), (1,), 1536, 512),
+        ((4, 5), (0,), 1536, 512),
         ((6, 7), (0,), 1536, 256),
         ((6, 7), (0,), 1792, 256),
     ],
@@ -84,11 +93,7 @@ def tile_ltcattentioncell_w_kernel(
         for d in range(4):
             wr = big.tile([P, 4, 2048], BF16, tag="big", name="wraw%d" % d, align_bytes=64)
             w_src = W_tau[512 * d : 512 * d + 512, :].rearrange("(p t) i -> p t i", t=4)
-            if d == 0:
-                nc.sync.dma_start(out=wr[:, :, 0:1024], in_=w_src[:, :, 0:1024])
-                nc.sync.dma_start(out=wr[:, :, 1024:2048], in_=w_src[:, :, 1024:2048])
-            else:
-                nc.sync.dma_start(out=wr[:], in_=w_src)
+            nc.sync.dma_start(out=wr[:], in_=w_src)
             wraw.append(wr)
             if d == 1:
                 nc.sync.dma_start(out=comb[:, 0:512], in_=x_t)
@@ -300,12 +305,99 @@ def tile_ltcattentioncell_w_kernel(
         tau_part1(3)
         broadcast_bgd()
 
+        banks = {}
+        done = {}
+        temps = {}
+
+        def consume_dma(k, j):
+            off = sum([2 * e[3] for e in TILES[k][:j]])
+            gs, halves, o0, width = TILES[k][j]
+            for gi in range(len(gs)):
+                g = gs[gi]
+                for gid in range(len(GROUPS)):
+                    half, s0, sw, tag = GROUPS[gid]
+                    if half not in halves or s0 < o0 or s0 + sw > o0 + width:
+                        continue
+                    if gid not in banks:
+                        pool = ps_a if tag == "A" else ps_b
+                        banks[gid] = pool.tile([P, 512], F32, tag=tag, name="acc%d" % gid)
+                    n_done = done.get(gid, 0)
+                    row = half if len(halves) == 2 else gi
+                    w0 = off + row * width + (s0 - o0)
+                    n0 = 2048 * half + s0
+                    kk = 4 * (g % 4)
+                    nc.tensor.matmul_mx(
+                        out=banks[gid][:, 0:sw],
+                        lhsT=codes[:, P * g : P * g + P].bitcast(FP8X4),
+                        lhsT_scale=ascl[:, P * g : P * g + P],
+                        rhs=wtiles[k][:, w0 : w0 + sw].bitcast(FP8X4),
+                        rhs_scale=planes[kk:P, g // 4, n0 : n0 + sw],
+                        start=(n_done == 0),
+                        stop=(n_done == 7),
+                    )
+                    done[gid] = n_done + 1
+
+        def consume_tile(k):
+            for j in range(len(TILES[k])):
+                consume_dma(k, j)
+
+        def ep_add(gid):
+            half, s0, sw, tag = GROUPS[gid]
+            tmp = ep.tile([P, 512], F32, tag="add%d" % half, name="add%d" % gid)
+            nc.vector.tensor_tensor(
+                out=tmp[:, 0:sw],
+                in0=banks[gid][:, 0:sw],
+                in1=bgd_b[:, 2048 * half + s0 : 2048 * half + s0 + sw],
+                op=ALU.add,
+            )
+            temps[gid] = tmp
+
+        def ep_tanh(gid):
+            half, s0, sw, tag = GROUPS[gid]
+            tmp = temps[gid]
+            nc.scalar.activation(
+                out=tmp[:, 0:sw], in_=tmp[:, 0:sw], func=ACT.Tanh, scale=(1.0 if half == 1 else 0.5)
+            )
+
+        def ep_w(gid):
+            half, s0, sw, tag = GROUPS[gid]
+            da = temps[gid]
+            nc.vector.tensor_tensor(
+                out=da[:, 0:sw], in0=da[:, 0:sw], in1=rr[:, s0 : s0 + sw], op=ALU.mult
+            )
+
+        def ep_out(gid, did):
+            half, s0, sw, tag = GROUPS[gid]
+            d0 = s0 - GROUPS[did][1]
+            da = temps[did]
+            ga = temps[gid]
+            ot = ep.tile([P, 512], F32, tag="ot", name="ot%d" % gid, bufs=5)
+            nc.vector.scalar_tensor_tensor(
+                out=ga[:, 0:sw],
+                in0=ga[:, 0:sw],
+                scalar=1.0,
+                in1=da[:, d0 : d0 + sw],
+                op0=ALU.add,
+                op1=ALU.mult,
+            )
+            nc.vector.tensor_tensor(
+                out=ot[:, 0:sw], in0=ga[:, 0:sw], in1=el[:, s0 : s0 + sw], op=ALU.subtract
+            )
+            nc.sync.dma_start(out=out[:, s0 : s0 + sw], in_=ot[:, 0:sw])
+
         blks = [slice(512 * d, 512 * d + 512) for d in range(4)]
         for blk in blks:
             nc.scalar.activation(out=el[:, blk], in_=el[:, blk], func=ACT.Ln, bias=1.0)
             nc.vector.tensor_tensor(out=rr[:, blk], in0=rr[:, blk], in1=el[:, blk], op=ALU.add)
         for blk in blks:
             nc.scalar.activation(out=rr[:, blk], in_=rr[:, blk], func=ACT.Ln, scale=2.0)
+        consume_tile(0)
+        issue_tile(7)
+        consume_tile(1)
+        consume_tile(2)
+        consume_tile(3)
+        for gid in range(4):
+            ep_add(gid)
         for d in range(4):
             blk = blks[d]
             nc.scalar.activation(out=rr[:, blk], in_=rr[:, blk], func=ACT.Exp, scale=-1.0)
@@ -317,108 +409,32 @@ def tile_ltcattentioncell_w_kernel(
                 op0=ALU.mult,
                 op1=ALU.mult,
             )
+        for gid in range(4):
+            ep_tanh(gid)
+        for did in (0, 2):
+            ep_w(did)
+            ep_out(did + 1, did)
 
-        banks = {}
-        done = {}
-        temps = {}
-
-        def consume_dma(k, j):
-            off = sum([2 * e[3] for e in TILES[k][:j]])
-            gs, halves, o0, width = TILES[k][j]
-            for gi in range(len(gs)):
-                g = gs[gi]
-                for si in range(len(SEGS)):
-                    s0, sw = SEGS[si]
-                    if s0 < o0 or s0 + sw > o0 + width:
-                        continue
-                    if si not in banks:
-                        pool = ps_a if SEG_TAG[si] == "A" else ps_b
-                        dps = pool.tile([P, 512], F32, tag=SEG_TAG[si], name="dps%d" % si)
-                        gps = pool.tile([P, 512], F32, tag=SEG_TAG[si], name="gps%d" % si)
-                        banks[si] = (gps, dps)
-                    for half in halves:
-                        n_done = done.get((si, half), 0)
-                        row = half if len(halves) == 2 else gi
-                        w0 = off + row * width + (s0 - o0)
-                        n0 = 2048 * half + s0
-                        kk = 4 * (g % 4)
-                        nc.tensor.matmul_mx(
-                            out=banks[si][half][:, 0:sw],
-                            lhsT=codes[:, P * g : P * g + P].bitcast(FP8X4),
-                            lhsT_scale=ascl[:, P * g : P * g + P],
-                            rhs=wtiles[k][:, w0 : w0 + sw].bitcast(FP8X4),
-                            rhs_scale=planes[kk:P, g // 4, n0 : n0 + sw],
-                            start=(n_done == 0),
-                            stop=(n_done == 7),
-                        )
-                        done[(si, half)] = n_done + 1
-
-        def consume_tile(k):
-            for j in range(len(TILES[k])):
-                consume_dma(k, j)
-
-        def ep_add(si, half):
-            s0, sw = SEGS[si]
-            tmp = ep.tile([P, 512], F32, tag="add%d" % half, name="add%d_%d" % (half, si))
-            nc.vector.tensor_tensor(
-                out=tmp[:, 0:sw],
-                in0=banks[si][half][:, 0:sw],
-                in1=bgd_b[:, 2048 * half + s0 : 2048 * half + s0 + sw],
-                op=ALU.add,
-            )
-            nc.scalar.activation(
-                out=tmp[:, 0:sw], in_=tmp[:, 0:sw], func=ACT.Tanh, scale=(1.0 if half == 1 else 0.5)
-            )
-            temps[(si, half)] = tmp
-
-        def ep_w(si):
-            s0, sw = SEGS[si]
-            da = temps[(si, 1)]
-            nc.vector.tensor_tensor(
-                out=da[:, 0:sw], in0=da[:, 0:sw], in1=rr[:, s0 : s0 + sw], op=ALU.mult
-            )
-
-        def ep_out(si, queue):
-            s0, sw = SEGS[si]
-            da = temps[(si, 1)]
-            ga = temps[(si, 0)]
-            ot = ep.tile([P, 512], F32, tag="ot", name="ot%d" % si)
-            nc.vector.scalar_tensor_tensor(
-                out=ga[:, 0:sw], in0=ga[:, 0:sw], scalar=1.0, in1=da[:, 0:sw], op0=ALU.add, op1=ALU.mult
-            )
-            nc.vector.tensor_tensor(
-                out=ot[:, 0:sw], in0=ga[:, 0:sw], in1=el[:, s0 : s0 + sw], op=ALU.subtract
-            )
-            queue.dma_start(out=out[:, s0 : s0 + sw], in_=ot[:, 0:sw])
-
-        consume_tile(0)
-        issue_tile(7)
-        consume_tile(1)
-        consume_tile(2)
-        consume_tile(3)
-        for si in (0, 1):
-            ep_add(si, 1)
-            ep_add(si, 0)
-        for si in (0, 1):
-            ep_w(si)
-            ep_out(si, nc.scalar)
         consume_tile(4)
         consume_tile(5)
         consume_tile(6)
-        ep_add(2, 1)
-        ep_add(2, 0)
-        ep_w(2)
-        ep_out(2, nc.sync)
+        ep_add(4)
+        ep_tanh(4)
+        ep_add(5)
+        ep_tanh(5)
+        ep_w(4)
+        ep_out(5, 4)
         consume_dma(7, 0)
         consume_dma(7, 1)
+        ep_add(6)
+        ep_tanh(6)
         consume_dma(7, 2)
-        ep_add(3, 1)
-        ep_add(4, 1)
-        ep_w(3)
-        ep_w(4)
         consume_dma(7, 3)
-        ep_add(3, 0)
-        ep_out(3, nc.sync)
+        ep_w(6)
+        ep_add(7)
+        ep_tanh(7)
         consume_dma(7, 4)
-        ep_add(4, 0)
-        ep_out(4, nc.sync)
+        ep_add(8)
+        ep_tanh(8)
+        ep_out(7, 6)
+        ep_out(8, 6)

@@ -63,6 +63,7 @@ def tile_ltcattentioncell_w_kernel(
         ident_f = const.tile([P, P], F32)
         ident_b = const.tile([P, P], BF16)
         rows = const.tile([P, P], BF16)
+        vecs = const.tile([P, 512], BF16)
         planes = const.tile([P, 2, 4096], U8, align_bytes=64)
         comb = const.tile([P, 4096], BF16, align_bytes=64)
         grouped = const.tile([P, 4096], BF16, align_bytes=64)
@@ -73,22 +74,22 @@ def tile_ltcattentioncell_w_kernel(
         c_b = const.tile([P, 2048], F32)
         el = const.tile([P, 2048], F32)
         rr = const.tile([P, 2048], F32)
-        stb = const.tile([P, 32], BF16)
         gc = const.tile([P, 32], F32)
         gl = const.tile([P, 32], F32)
         sp = const.tile([P, 32], F32)
         c_t = const.tile([P, 16], F32)
 
+        nc.vector.memset(vecs[:], 0.0)
         nc.vector.memset(rows[:], 0.0)
         nc.vector.memset(planes[:].rearrange("p a n -> p (a n)").bitcast(I32), 0)
         make_identity(nc, ident_f[:])
         make_identity(nc, ident_b[:])
 
         nc.sync.dma_start(out=comb[:, 512:2560], in_=h_ltc)
-        nc.scalar.dma_start(out=rows[0:32, :], in_=b_gd.rearrange("(r c) -> r c", c=P))
-        nc.scalar.dma_start(out=rows[32:48, :], in_=b_tau.rearrange("(r c) -> r c", c=P))
-        nc.scalar.dma_start(out=rows[48:64, :], in_=gleak.rearrange("(r c) -> r c", c=P))
-        nc.scalar.dma_start(out=rows[64:80, :], in_=cm.rearrange("(r c) -> r c", c=P))
+        nc.scalar.dma_start(out=vecs[0:8, :], in_=b_gd.rearrange("(r c) -> r c", c=512))
+        nc.scalar.dma_start(out=vecs[8:12, :], in_=b_tau.rearrange("(r c) -> r c", c=512))
+        nc.scalar.dma_start(out=rows[0:16, :], in_=gleak.rearrange("(r c) -> r c", c=P))
+        nc.scalar.dma_start(out=rows[16:32, :], in_=cm.rearrange("(r c) -> r c", c=P))
         wraw = []
         for d in range(4):
             wr = big.tile([P, 4, 2048], BF16, tag="big", name="wraw%d" % d, align_bytes=64)
@@ -133,6 +134,24 @@ def tile_ltcattentioncell_w_kernel(
         for k in range(3):
             issue_tile(k)
 
+        def spread_row(dst, row, start, stop):
+            nc.tensor.matmul(
+                out=dst, lhsT=ident_b[:, row : row + 1].to_broadcast([P, P]), rhs=vecs[:], start=start, stop=stop
+            )
+
+        tau_ps = []
+        for d in range(4):
+            tau_ps.append(ps_b.tile([P, 512], F32, tag="B", name="tau%d" % d))
+            spread_row(tau_ps[d][:], 8 + d, True, False)
+        for k in range(4):
+            bps = ps_a.tile([P, 1024], BF16, tag="A", name="bps%d" % k)
+            for jj in range(2):
+                spread_row(bps[:, 512 * jj : 512 * jj + 512], 2 * k + jj, True, True)
+            if k % 2 == 0:
+                nc.vector.tensor_copy(out=bgd_b[:, 1024 * k : 1024 * k + 1024], in_=bps[:])
+            else:
+                nc.scalar.copy(out=bgd_b[:, 1024 * k : 1024 * k + 1024], in_=bps[:])
+
         combw = comb[:].bitcast(F32)
         for k in range(2):
             hps = ps_a.tile([P, 4, P], F32, tag="A", name="hps%d" % k)
@@ -149,11 +168,10 @@ def tile_ltcattentioncell_w_kernel(
 
         gview = grouped[:].bitcast(F32).rearrange("p (g b u) -> p g b u", g=8, u=2)
 
-        def transpose_combined():
-            for k in range(4):
-                xg = ps_a.tile([P, 2, 2, P], F32, tag="A", name="xg%d" % k)
-                for gi in range(2):
-                    g = 2 * k + gi
+        def transpose_combined(pairs):
+            for k, (g0, g1) in enumerate(pairs):
+                xg = ps_a.tile([P, 2, 2, P], F32, tag="A", name="xg%d_%d" % (g0, g1))
+                for gi, g in enumerate((g0, g1)):
                     for u in range(2):
                         nc.tensor.transpose(
                             out=xg[:, gi, u, :],
@@ -161,10 +179,11 @@ def tile_ltcattentioncell_w_kernel(
                             identity=ident_f[:],
                         )
                 src = xg[:].rearrange("p g u b -> p g b u")
+                dst = gview[:, g0 : g1 + 1 : g1 - g0]
                 if k % 2 == 0:
-                    nc.vector.tensor_copy(out=gview[:, 2 * k : 2 * k + 2], in_=src)
+                    nc.vector.tensor_copy(out=dst, in_=src)
                 else:
-                    nc.scalar.copy(out=gview[:, 2 * k : 2 * k + 2], in_=src)
+                    nc.scalar.copy(out=dst, in_=src)
 
         def quantise_combined():
             for half in range(2):
@@ -176,17 +195,15 @@ def tile_ltcattentioncell_w_kernel(
 
         st_ps = ps_a.tile([P, P], BF16, tag="A", name="st_ps")
         nc.tensor.transpose(out=st_ps[:], in_=rows[:], identity=ident_b[:])
-        nc.vector.tensor_copy(out=gc[:], in_=st_ps[:, 48:80])
-        nc.vector.tensor_copy(out=stb[:], in_=st_ps[:, 0:32])
-        nc.scalar.activation(out=gl[:], in_=gc[:], func=ACT.Abs)
-        nc.scalar.activation(out=gl[:], in_=gl[:], func=ACT.Exp, scale=-1.0)
-        nc.scalar.activation(out=gl[:], in_=gl[:], func=ACT.Ln, bias=1.0)
-        nc.vector.scalar_tensor_tensor(
-            out=sp[:], in0=gc[:], scalar=0.0, in1=gl[:], op0=ALU.max, op1=ALU.add
-        )
-        nc.vector.scalar_tensor_tensor(
-            out=c_t[:], in0=sp[:, 0:16], scalar=1e-6, in1=sp[:, 16:32], op0=ALU.add, op1=ALU.add
-        )
+        nc.vector.tensor_copy(out=gc[:], in_=st_ps[:, 0:32])
+
+        def finish_c():
+            nc.vector.scalar_tensor_tensor(
+                out=sp[:], in0=gc[:], scalar=0.0, in1=gl[:], op0=ALU.max, op1=ALU.add
+            )
+            nc.vector.scalar_tensor_tensor(
+                out=c_t[:], in0=sp[:, 0:16], scalar=1e-6, in1=sp[:, 16:32], op0=ALU.add, op1=ALU.add
+            )
 
         def broadcast_c():
             for k in range(4):
@@ -204,25 +221,13 @@ def tile_ltcattentioncell_w_kernel(
                 else:
                     nc.scalar.copy(out=c_b[:, 512 * k : 512 * k + 512], in_=src)
 
-        def broadcast_bgd():
-            for k in range(4):
-                bps = ps_a.tile([P, 8, P], BF16, tag="A", name="bps%d" % k)
-                for jj in range(8):
-                    col = 8 * k + jj
-                    nc.tensor.transpose(
-                        out=bps[:, jj, :],
-                        in_=stb[:, col : col + 1].to_broadcast([P, P]),
-                        identity=ident_b[:],
-                    )
-                src = bps[:].rearrange("p j n -> p (j n)")
-                if k % 2 == 0:
-                    nc.vector.tensor_copy(out=bgd_b[:, 1024 * k : 1024 * k + 1024], in_=src)
-                else:
-                    nc.scalar.copy(out=bgd_b[:, 1024 * k : 1024 * k + 1024], in_=src)
+        transpose_combined(((1, 2), (3, 4)))
+        nc.scalar.activation(out=gl[:], in_=gc[:], func=ACT.Abs)
+        nc.scalar.activation(out=gl[:], in_=gl[:], func=ACT.Exp, scale=-1.0)
+        nc.scalar.activation(out=gl[:], in_=gl[:], func=ACT.Ln, bias=1.0)
 
         tps = {}
         wts = {}
-        tau_ps = []
 
         def unit_transposes(u, which):
             d, c = divmod(u, 8)
@@ -246,27 +251,14 @@ def tile_ltcattentioncell_w_kernel(
 
         def unit_matmul(u, e):
             d, c = divmod(u, 8)
-            if c == 0 and e == 0:
-                tau_ps.append(ps_b.tile([P, 512], F32, tag="B", name="tau%d" % d))
             rhs = wts[u][:].bitcast(BF16).rearrange("q (o e) -> q o e", e=2)[:, :, e]
             nc.tensor.matmul(
                 out=tau_ps[d][:],
                 lhsT=h_t[:, c, e, :],
                 rhs=rhs,
-                start=(c == 0 and e == 0),
+                start=False,
                 stop=(c == 7 and e == 1),
             )
-
-        def tau_bias(d):
-            for jj in range(4):
-                r = 32 + 4 * d + jj
-                nc.tensor.matmul(
-                    out=tau_ps[d][:, P * jj : P * jj + P],
-                    lhsT=ident_b[:, r : r + 1].to_broadcast([P, P]),
-                    rhs=rows[:],
-                    start=False,
-                    stop=False,
-                )
 
         def tau_part1(d):
             blk = slice(512 * d, 512 * d + 512)
@@ -288,22 +280,21 @@ def tile_ltcattentioncell_w_kernel(
             if nxt < 32:
                 unit_transposes(nxt, (2, 3))
             unit_matmul(u, 1)
-            if u % 8 == 2:
-                tau_bias(u // 8)
             if nxt < 32:
                 unit_copy(nxt)
             if u % 8 == 4:
                 issue_tile(3 + u // 8)
+            if u == 3:
+                finish_c()
             if u == 6:
                 broadcast_c()
             if u == 14:
-                transpose_combined()
+                transpose_combined(((0, 5), (6, 7)))
             if u == 17:
                 quantise_combined()
             if u >= 9 and (u - 9) % 8 == 0:
                 tau_part1((u - 9) // 8)
         tau_part1(3)
-        broadcast_bgd()
 
         banks = {}
         done = {}

@@ -16,34 +16,24 @@ P = 128
 FLOPS = 2 * 128 * 4096 * 4096 + 2 * 128 * 2048 * 2048
 
 PINNED = True
-BOTH = (1, 0)
-GROUPS = [
-    (1, 0, 512, "B"),
-    (0, 0, 512, "B"),
-    (1, 512, 512, "B"),
-    (0, 512, 512, "B"),
-    (1, 1024, 512, "A"),
-    (0, 1024, 512, "A"),
-    (1, 1536, 512, "A"),
-    (0, 1536, 256, "A"),
-    (0, 1792, 256, "B"),
-]
-TILES = [
-    [((0,), BOTH, 0, 1024), ((1,), BOTH, 0, 1024)],
-    [((2,), BOTH, 0, 1024), ((3,), BOTH, 0, 1024)],
-    [((4,), BOTH, 0, 1024), ((5,), BOTH, 0, 1024)],
-    [((6,), BOTH, 0, 1024), ((7,), BOTH, 0, 1024)],
-    [((0,), BOTH, 1024, 1024), ((1,), BOTH, 1024, 1024)],
-    [((2,), BOTH, 1024, 1024), ((3,), BOTH, 1024, 1024)],
-    [((4,), BOTH, 1024, 512), ((5,), BOTH, 1024, 512), ((6,), BOTH, 1024, 512), ((7,), BOTH, 1024, 512)],
-    [
-        ((4, 5), (1,), 1536, 512),
-        ((6, 7), (1,), 1536, 512),
-        ((4, 5), (0,), 1536, 512),
-        ((6, 7), (0,), 1536, 256),
-        ((6, 7), (0,), 1792, 256),
-    ],
-]
+GROUPS = (
+    [(1, 512 * d, 512, "A") for d in range(4)]
+    + [(0, 512 * d, 512, "B") for d in range(3)]
+    + [(0, 1536, 256, "B"), (0, 1792, 256, "A")]
+)
+TILES = (
+    [[((2 * i,), 1, 0, 2048), ((2 * i + 1,), 1, 0, 2048)] for i in range(4)]
+    + [[((4 * i, 4 * i + 1), 0, 0, 1024), ((4 * i + 2, 4 * i + 3), 0, 0, 1024)] for i in range(2)]
+    + [[((0, 1, 2, 3), 0, 1024, 512), ((4, 5, 6, 7), 0, 1024, 512)]]
+    + [
+        [
+            ((0, 1, 2, 3), 0, 1536, 512),
+            ((4, 5), 0, 1536, 512),
+            ((6, 7), 0, 1536, 256),
+            ((6, 7), 0, 1792, 256),
+        ]
+    ]
+)
 
 
 def tile_ltcattentioncell_w_kernel(
@@ -86,10 +76,10 @@ def tile_ltcattentioncell_w_kernel(
         make_identity(nc, ident_b[:])
 
         nc.sync.dma_start(out=comb[:, 512:2560], in_=h_ltc)
-        nc.scalar.dma_start(out=vecs[0:8, :], in_=b_gd.rearrange("(r c) -> r c", c=512))
-        nc.scalar.dma_start(out=vecs[8:12, :], in_=b_tau.rearrange("(r c) -> r c", c=512))
-        nc.scalar.dma_start(out=rows[0:16, :], in_=gleak.rearrange("(r c) -> r c", c=P))
-        nc.scalar.dma_start(out=rows[16:32, :], in_=cm.rearrange("(r c) -> r c", c=P))
+        nc.sync.dma_start(out=vecs[0:8, :], in_=b_gd.rearrange("(r c) -> r c", c=512))
+        nc.sync.dma_start(out=vecs[8:12, :], in_=b_tau.rearrange("(r c) -> r c", c=512))
+        nc.sync.dma_start(out=rows[0:16, :], in_=gleak.rearrange("(r c) -> r c", c=P))
+        nc.sync.dma_start(out=rows[16:32, :], in_=cm.rearrange("(r c) -> r c", c=P))
         wraw = []
         for d in range(4):
             wr = big.tile([P, 4, 2048], BF16, tag="big", name="wraw%d" % d, align_bytes=64)
@@ -111,24 +101,16 @@ def tile_ltcattentioncell_w_kernel(
         def issue_tile(k):
             wt = big.tile([P, 4096], U32, tag="big", name="wgd%d" % k, align_bytes=64)
             off = 0
-            for gs, halves, o0, width in TILES[k]:
-                if len(halves) == 2:
-                    src = (
-                        W_gd_words[gs[0]]
-                        .rearrange("p n t -> p (n t)")
-                        .rearrange("p (s m) -> p s m", s=2)[:, :, 4 * o0 : 4 * (o0 + width)]
-                        .bitcast(I32)
-                    )
-                else:
-                    n0 = 2048 * halves[0] + o0
-                    src = (
-                        W_gd_words[gs[0] : gs[0] + len(gs)]
-                        .rearrange("g p n t -> p g (n t)")[:, :, 4 * n0 : 4 * (n0 + width)]
-                        .bitcast(I32)
-                    )
-                dst = wt[:, off : off + 2 * width].rearrange("p (s m) -> p s m", s=2).bitcast(I32)
-                nc.sync.dma_start(out=dst, in_=src)
-                off += 2 * width
+            for gs, half, o0, width in TILES[k]:
+                n0 = 2048 * half + o0
+                words = len(gs) * width
+                nc.sync.dma_start(
+                    out=wt[:, off : off + words].rearrange("p (g m) -> p g m", g=len(gs)).bitcast(I32),
+                    in_=W_gd_words[gs[0] : gs[0] + len(gs)]
+                    .rearrange("g p n t -> p g (n t)")[:, :, 4 * n0 : 4 * (n0 + width)]
+                    .bitcast(I32),
+                )
+                off += words
             wtiles[k] = wt
 
         for k in range(3):
@@ -301,20 +283,17 @@ def tile_ltcattentioncell_w_kernel(
         temps = {}
 
         def consume_dma(k, j):
-            off = sum([2 * e[3] for e in TILES[k][:j]])
-            gs, halves, o0, width = TILES[k][j]
-            for gi in range(len(gs)):
-                g = gs[gi]
-                for gid in range(len(GROUPS)):
-                    half, s0, sw, tag = GROUPS[gid]
-                    if half not in halves or s0 < o0 or s0 + sw > o0 + width:
+            off = sum([len(e[0]) * e[3] for e in TILES[k][:j]])
+            gs, half, o0, width = TILES[k][j]
+            for gi, g in enumerate(gs):
+                for gid, (ghalf, s0, sw, tag) in enumerate(GROUPS):
+                    if ghalf != half or s0 < o0 or s0 + sw > o0 + width:
                         continue
                     if gid not in banks:
                         pool = ps_a if tag == "A" else ps_b
                         banks[gid] = pool.tile([P, 512], F32, tag=tag, name="acc%d" % gid)
                     n_done = done.get(gid, 0)
-                    row = half if len(halves) == 2 else gi
-                    w0 = off + row * width + (s0 - o0)
+                    w0 = off + gi * width + (s0 - o0)
                     n0 = 2048 * half + s0
                     kk = 4 * (g % 4)
                     nc.tensor.matmul_mx(
@@ -334,7 +313,8 @@ def tile_ltcattentioncell_w_kernel(
 
         def ep_add(gid):
             half, s0, sw, tag = GROUPS[gid]
-            tmp = ep.tile([P, 512], F32, tag="add%d" % half, name="add%d" % gid)
+            bufs = 4 if half == 1 else 3
+            tmp = ep.tile([P, 512], F32, tag="add%d" % half, name="add%d" % gid, bufs=bufs)
             nc.vector.tensor_tensor(
                 out=tmp[:, 0:sw],
                 in0=banks[gid][:, 0:sw],
@@ -357,12 +337,13 @@ def tile_ltcattentioncell_w_kernel(
                 out=da[:, 0:sw], in0=da[:, 0:sw], in1=rr[:, s0 : s0 + sw], op=ALU.mult
             )
 
-        def ep_out(gid, did):
+        def ep_out(gid):
             half, s0, sw, tag = GROUPS[gid]
-            d0 = s0 - GROUPS[did][1]
+            did = s0 // 512
+            d0 = s0 - 512 * did
             da = temps[did]
             ga = temps[gid]
-            ot = ep.tile([P, 512], F32, tag="ot", name="ot%d" % gid, bufs=5)
+            ot = ep.tile([P, 512], F32, tag="ot", name="ot%d" % gid, bufs=4)
             nc.vector.scalar_tensor_tensor(
                 out=ga[:, 0:sw],
                 in0=ga[:, 0:sw],
@@ -384,9 +365,8 @@ def tile_ltcattentioncell_w_kernel(
             nc.scalar.activation(out=rr[:, blk], in_=rr[:, blk], func=ACT.Ln, scale=2.0)
         consume_tile(0)
         issue_tile(7)
-        consume_tile(1)
-        consume_tile(2)
-        consume_tile(3)
+        for k in range(1, 4):
+            consume_tile(k)
         for gid in range(4):
             ep_add(gid)
         for d in range(4):
@@ -402,30 +382,25 @@ def tile_ltcattentioncell_w_kernel(
             )
         for gid in range(4):
             ep_tanh(gid)
-        for did in (0, 2):
-            ep_w(did)
-            ep_out(did + 1, did)
+            ep_w(gid)
 
         consume_tile(4)
         consume_tile(5)
+        for gid in (4, 5):
+            ep_add(gid)
+            ep_tanh(gid)
+        for gid in (4, 5):
+            ep_out(gid)
         consume_tile(6)
-        ep_add(4)
-        ep_tanh(4)
-        ep_add(5)
-        ep_tanh(5)
-        ep_w(4)
-        ep_out(5, 4)
-        consume_dma(7, 0)
-        consume_dma(7, 1)
         ep_add(6)
         ep_tanh(6)
-        consume_dma(7, 2)
-        consume_dma(7, 3)
-        ep_w(6)
+        ep_out(6)
+        for j in range(3):
+            consume_dma(7, j)
         ep_add(7)
         ep_tanh(7)
-        consume_dma(7, 4)
+        consume_dma(7, 3)
         ep_add(8)
         ep_tanh(8)
-        ep_out(7, 6)
-        ep_out(8, 6)
+        ep_out(7)
+        ep_out(8)

from contextlib import ExitStack

import concourse.mybir as mybir
from concourse.masks import make_identity

F32 = mybir.dt.float32
BF16 = mybir.dt.bfloat16
U32 = mybir.dt.uint32
U8 = mybir.dt.uint8
I32 = mybir.dt.int32
FP8X4 = mybir.dt.float8_e4m3fn_x4
ALU = mybir.AluOpType
ACT = mybir.ActivationFunctionType

P = 128
FLOPS = 2 * 128 * 4096 * 4096 + 2 * 128 * 2048 * 2048

PINNED = True
GROUPS = (
    [(1, 512 * d, 512, "A") for d in range(4)]
    + [(0, 512 * d, 512, "B") for d in range(3)]
    + [(0, 1536, 256, "B"), (0, 1792, 256, "A")]
)
TILES = (
    [[((2 * i,), 1, 0, 2048), ((2 * i + 1,), 1, 0, 2048)] for i in range(4)]
    + [[((4 * i, 4 * i + 1), 0, 0, 1024), ((4 * i + 2, 4 * i + 3), 0, 0, 1024)] for i in range(2)]
    + [[((0, 1, 2, 3), 0, 1024, 512), ((4, 5, 6, 7), 0, 1024, 512)]]
    + [
        [
            ((0, 1, 2, 3), 0, 1536, 512),
            ((4, 5), 0, 1536, 512),
            ((6, 7), 0, 1536, 256),
            ((6, 7), 0, 1792, 256),
        ]
    ]
)


def tile_ltcattentioncell_w_kernel(
    tc, t, h_ltc, x_t, context, W_gd_words, W_gd_scales, b_gd, W_tau, b_tau, gleak, cm, out
):
    nc = tc.nc
    with ExitStack() as ctx:
        const = ctx.enter_context(tc.tile_pool(name="const", bufs=1))
        big = ctx.enter_context(tc.tile_pool(name="big", bufs=7))
        wtp = ctx.enter_context(tc.tile_pool(name="wtp", bufs=6))
        ep = ctx.enter_context(tc.tile_pool(name="ep", bufs=3))
        ps_a = ctx.enter_context(tc.psum_pool(name="psa", bufs=4))
        ps_b = ctx.enter_context(tc.psum_pool(name="psb", bufs=4))
        if PINNED:
            ctx.enter_context(tc.manual_schedule())

        ident_f = const.tile([P, P], F32)
        ident_b = const.tile([P, P], BF16)
        rows = const.tile([P, P], BF16)
        vecs = const.tile([P, 512], BF16)
        planes = const.tile([P, 2, 4096], U8, align_bytes=64)
        comb = const.tile([P, 4096], BF16, align_bytes=64)
        grouped = const.tile([P, 4096], BF16, align_bytes=64)
        codes = const.tile([P, 1024], U32, align_bytes=64)
        ascl = const.tile([P, 1024], U8, align_bytes=64)
        h_t = const.tile([P, 8, 2, P], BF16)
        bgd_b = const.tile([P, 4096], BF16)
        c_b = const.tile([P, 2048], F32)
        el = const.tile([P, 2048], F32)
        rr = const.tile([P, 2048], F32)
        gc = const.tile([P, 32], F32)
        gl = const.tile([P, 32], F32)
        sp = const.tile([P, 32], F32)
        c_t = const.tile([P, 16], F32)

        nc.vector.memset(vecs[:], 0.0)
        nc.vector.memset(rows[:], 0.0)
        nc.vector.memset(planes[:].rearrange("p a n -> p (a n)").bitcast(I32), 0)
        make_identity(nc, ident_f[:])
        make_identity(nc, ident_b[:])

        nc.sync.dma_start(out=comb[:, 512:2560], in_=h_ltc)
        nc.sync.dma_start(out=vecs[0:8, :], in_=b_gd.rearrange("(r c) -> r c", c=512))
        nc.sync.dma_start(out=vecs[8:12, :], in_=b_tau.rearrange("(r c) -> r c", c=512))
        nc.sync.dma_start(out=rows[0:16, :], in_=gleak.rearrange("(r c) -> r c", c=P))
        nc.sync.dma_start(out=rows[16:32, :], in_=cm.rearrange("(r c) -> r c", c=P))
        wraw = []
        for d in range(4):
            wr = big.tile([P, 4, 2048], BF16, tag="big", name="wraw%d" % d, align_bytes=64)
            w_src = W_tau[512 * d : 512 * d + 512, :].rearrange("(p t) i -> p t i", t=4)
            nc.sync.dma_start(out=wr[:], in_=w_src)
            wraw.append(wr)
            if d == 1:
                nc.sync.dma_start(out=comb[:, 0:512], in_=x_t)
                nc.sync.dma_start(out=comb[:, 2560:4096], in_=context)
        for a in range(2):
            for q in (0, 2, 1, 3):
                nc.sync.dma_start(
                    out=planes[32 * q : 32 * q + 16, a, :].bitcast(I32),
                    in_=W_gd_scales[4 * a : 4 * a + 4, 4 * q : 4 * q + 4, :].bitcast(I32),
                )

        wtiles = {}

        def issue_tile(k):
            wt = big.tile([P, 4096], U32, tag="big", name="wgd%d" % k, align_bytes=64)
            off = 0
            for gs, half, o0, width in TILES[k]:
                n0 = 2048 * half + o0
                words = len(gs) * width
                nc.sync.dma_start(
                    out=wt[:, off : off + words].rearrange("p (g m) -> p g m", g=len(gs)).bitcast(I32),
                    in_=W_gd_words[gs[0] : gs[0] + len(gs)]
                    .rearrange("g p n t -> p g (n t)")[:, :, 4 * n0 : 4 * (n0 + width)]
                    .bitcast(I32),
                )
                off += words
            wtiles[k] = wt

        for k in range(3):
            issue_tile(k)

        def spread_row(dst, row, start, stop):
            nc.tensor.matmul(
                out=dst, lhsT=ident_b[:, row : row + 1].to_broadcast([P, P]), rhs=vecs[:], start=start, stop=stop
            )

        tau_ps = []
        for d in range(4):
            tau_ps.append(ps_b.tile([P, 512], F32, tag="B", name="tau%d" % d))
            spread_row(tau_ps[d][:], 8 + d, True, False)
        for k in range(4):
            bps = ps_a.tile([P, 1024], BF16, tag="A", name="bps%d" % k)
            for jj in range(2):
                spread_row(bps[:, 512 * jj : 512 * jj + 512], 2 * k + jj, True, True)
            if k % 2 == 0:
                nc.vector.tensor_copy(out=bgd_b[:, 1024 * k : 1024 * k + 1024], in_=bps[:])
            else:
                nc.scalar.copy(out=bgd_b[:, 1024 * k : 1024 * k + 1024], in_=bps[:])

        combw = comb[:].bitcast(F32)
        for k in range(2):
            hps = ps_a.tile([P, 4, P], F32, tag="A", name="hps%d" % k)
            for cc in range(4):
                c = 4 * k + cc
                nc.tensor.transpose(
                    out=hps[:, cc, :], in_=combw[:, 256 + P * c : 256 + P * c + P], identity=ident_f[:]
                )
            src = hps[:].bitcast(BF16).rearrange("q c (b e) -> q c e b", e=2)
            if k == 0:
                nc.vector.tensor_copy(out=h_t[:, 0:4, :, :], in_=src)
            else:
                nc.scalar.copy(out=h_t[:, 4:8, :, :], in_=src)

        gview = grouped[:].bitcast(F32).rearrange("p (g b u) -> p g b u", g=8, u=2)

        def transpose_combined(pairs):
            for k, (g0, g1) in enumerate(pairs):
                xg = ps_a.tile([P, 2, 2, P], F32, tag="A", name="xg%d_%d" % (g0, g1))
                for gi, g in enumerate((g0, g1)):
                    for u in range(2):
                        nc.tensor.transpose(
                            out=xg[:, gi, u, :],
                            in_=combw[:, 256 * g + u : 256 * (g + 1) : 2],
                            identity=ident_f[:],
                        )
                src = xg[:].rearrange("p g u b -> p g b u")
                dst = gview[:, g0 : g1 + 1 : g1 - g0]
                if k % 2 == 0:
                    nc.vector.tensor_copy(out=dst, in_=src)
                else:
                    nc.scalar.copy(out=dst, in_=src)

        def quantise_combined():
            for half in range(2):
                nc.vector.quantize_mx(
                    out=codes[:, 512 * half : 512 * half + 512].bitcast(FP8X4),
                    scales=ascl[:, 512 * half : 512 * half + 512],
                    in_=grouped[:, 2048 * half : 2048 * half + 2048],
                )

        st_ps = ps_a.tile([P, P], BF16, tag="A", name="st_ps")
        nc.tensor.transpose(out=st_ps[:], in_=rows[:], identity=ident_b[:])
        nc.vector.tensor_copy(out=gc[:], in_=st_ps[:, 0:32])

        def finish_c():
            nc.vector.scalar_tensor_tensor(
                out=sp[:], in0=gc[:], scalar=0.0, in1=gl[:], op0=ALU.max, op1=ALU.add
            )
            nc.vector.scalar_tensor_tensor(
                out=c_t[:], in0=sp[:, 0:16], scalar=1e-6, in1=sp[:, 16:32], op0=ALU.add, op1=ALU.add
            )

        def broadcast_c():
            for k in range(4):
                cps = ps_a.tile([P, 4, P], F32, tag="A", name="cps%d" % k)
                for jj in range(4):
                    col = 4 * k + jj
                    nc.tensor.transpose(
                        out=cps[:, jj, :],
                        in_=c_t[:, col : col + 1].to_broadcast([P, P]),
                        identity=ident_f[:],
                    )
                src = cps[:].rearrange("p j n -> p (j n)")
                if k % 2 == 0:
                    nc.vector.tensor_copy(out=c_b[:, 512 * k : 512 * k + 512], in_=src)
                else:
                    nc.scalar.copy(out=c_b[:, 512 * k : 512 * k + 512], in_=src)

        transpose_combined(((1, 2), (3, 4)))
        nc.scalar.activation(out=gl[:], in_=gc[:], func=ACT.Abs)
        nc.scalar.activation(out=gl[:], in_=gl[:], func=ACT.Exp, scale=-1.0)
        nc.scalar.activation(out=gl[:], in_=gl[:], func=ACT.Ln, bias=1.0)

        tps = {}
        wts = {}

        def unit_transposes(u, which):
            d, c = divmod(u, 8)
            if u not in tps:
                tps[u] = ps_a.tile([P, 4, P], F32, tag="A", name="tp%d" % u)
            words = wraw[d][:].bitcast(F32)
            for tt in which:
                nc.tensor.transpose(
                    out=tps[u][:, tt, :], in_=words[:, tt, P * c : P * c + P], identity=ident_f[:]
                )

        def unit_copy(u):
            wt = wtp.tile([P, 512], F32, tag="wt", name="wt%d" % u)
            dst = wt[:].rearrange("q (p t) -> q p t", t=4)
            src = tps[u][:].rearrange("q t p -> q p t")
            if u % 2 == 0 and u >= 8:
                nc.scalar.copy(out=dst, in_=src)
            else:
                nc.vector.tensor_copy(out=dst, in_=src)
            wts[u] = wt

        def unit_matmul(u, e):
            d, c = divmod(u, 8)
            rhs = wts[u][:].bitcast(BF16).rearrange("q (o e) -> q o e", e=2)[:, :, e]
            nc.tensor.matmul(
                out=tau_ps[d][:],
                lhsT=h_t[:, c, e, :],
                rhs=rhs,
                start=False,
                stop=(c == 7 and e == 1),
            )

        def tau_part1(d):
            blk = slice(512 * d, 512 * d + 512)
            nc.scalar.activation(out=el[:, blk], in_=tau_ps[d][:], func=ACT.Abs)
            nc.vector.scalar_tensor_tensor(
                out=rr[:, blk], in0=tau_ps[d][:], scalar=0.0, in1=c_b[:, blk], op0=ALU.max, op1=ALU.add
            )
            nc.scalar.activation(out=el[:, blk], in_=el[:, blk], func=ACT.Exp, scale=-1.0)

        AHEAD = 3
        for u in range(AHEAD):
            unit_transposes(u, (0, 1, 2, 3))
            unit_copy(u)
        for u in range(32):
            nxt = u + AHEAD
            if nxt < 32:
                unit_transposes(nxt, (0, 1))
            unit_matmul(u, 0)
            if nxt < 32:
                unit_transposes(nxt, (2, 3))
            unit_matmul(u, 1)
            if nxt < 32:
                unit_copy(nxt)
            if u % 8 == 4:
                issue_tile(3 + u // 8)
            if u == 3:
                finish_c()
            if u == 6:
                broadcast_c()
            if u == 14:
                transpose_combined(((0, 5), (6, 7)))
            if u == 17:
                quantise_combined()
            if u >= 9 and (u - 9) % 8 == 0:
                tau_part1((u - 9) // 8)
        tau_part1(3)

        banks = {}
        done = {}
        temps = {}

        def consume_dma(k, j):
            off = sum([len(e[0]) * e[3] for e in TILES[k][:j]])
            gs, half, o0, width = TILES[k][j]
            for gi, g in enumerate(gs):
                for gid, (ghalf, s0, sw, tag) in enumerate(GROUPS):
                    if ghalf != half or s0 < o0 or s0 + sw > o0 + width:
                        continue
                    if gid not in banks:
                        pool = ps_a if tag == "A" else ps_b
                        banks[gid] = pool.tile([P, 512], F32, tag=tag, name="acc%d" % gid)
                    n_done = done.get(gid, 0)
                    w0 = off + gi * width + (s0 - o0)
                    n0 = 2048 * half + s0
                    kk = 4 * (g % 4)
                    nc.tensor.matmul_mx(
                        out=banks[gid][:, 0:sw],
                        lhsT=codes[:, P * g : P * g + P].bitcast(FP8X4),
                        lhsT_scale=ascl[:, P * g : P * g + P],
                        rhs=wtiles[k][:, w0 : w0 + sw].bitcast(FP8X4),
                        rhs_scale=planes[kk:P, g // 4, n0 : n0 + sw],
                        start=(n_done == 0),
                        stop=(n_done == 7),
                    )
                    done[gid] = n_done + 1

        def consume_tile(k):
            for j in range(len(TILES[k])):
                consume_dma(k, j)

        def ep_add(gid):
            half, s0, sw, tag = GROUPS[gid]
            bufs = 4 if half == 1 else 3
            tmp = ep.tile([P, 512], F32, tag="add%d" % half, name="add%d" % gid, bufs=bufs)
            nc.vector.tensor_tensor(
                out=tmp[:, 0:sw],
                in0=banks[gid][:, 0:sw],
                in1=bgd_b[:, 2048 * half + s0 : 2048 * half + s0 + sw],
                op=ALU.add,
            )
            temps[gid] = tmp

        def ep_tanh(gid):
            half, s0, sw, tag = GROUPS[gid]
            tmp = temps[gid]
            nc.scalar.activation(
                out=tmp[:, 0:sw], in_=tmp[:, 0:sw], func=ACT.Tanh, scale=(1.0 if half == 1 else 0.5)
            )

        def ep_w(gid):
            half, s0, sw, tag = GROUPS[gid]
            da = temps[gid]
            nc.vector.tensor_tensor(
                out=da[:, 0:sw], in0=da[:, 0:sw], in1=rr[:, s0 : s0 + sw], op=ALU.mult
            )

        def ep_out(gid):
            half, s0, sw, tag = GROUPS[gid]
            did = s0 // 512
            d0 = s0 - 512 * did
            da = temps[did]
            ga = temps[gid]
            ot = ep.tile([P, 512], F32, tag="ot", name="ot%d" % gid, bufs=4)
            nc.vector.scalar_tensor_tensor(
                out=ga[:, 0:sw],
                in0=ga[:, 0:sw],
                scalar=1.0,
                in1=da[:, d0 : d0 + sw],
                op0=ALU.add,
                op1=ALU.mult,
            )
            nc.vector.tensor_tensor(
                out=ot[:, 0:sw], in0=ga[:, 0:sw], in1=el[:, s0 : s0 + sw], op=ALU.subtract
            )
            nc.sync.dma_start(out=out[:, s0 : s0 + sw], in_=ot[:, 0:sw])

        blks = [slice(512 * d, 512 * d + 512) for d in range(4)]
        for blk in blks:
            nc.scalar.activation(out=el[:, blk], in_=el[:, blk], func=ACT.Ln, bias=1.0)
            nc.vector.tensor_tensor(out=rr[:, blk], in0=rr[:, blk], in1=el[:, blk], op=ALU.add)
        for blk in blks:
            nc.scalar.activation(out=rr[:, blk], in_=rr[:, blk], func=ACT.Ln, scale=2.0)
        consume_tile(0)
        issue_tile(7)
        for k in range(1, 4):
            consume_tile(k)
        for gid in range(4):
            ep_add(gid)
        for d in range(4):
            blk = blks[d]
            nc.scalar.activation(out=rr[:, blk], in_=rr[:, blk], func=ACT.Exp, scale=-1.0)
            nc.vector.scalar_tensor_tensor(
                out=el[:, blk],
                in0=comb[:, 512 + 512 * d : 1024 + 512 * d],
                scalar=2.0,
                in1=rr[:, blk],
                op0=ALU.mult,
                op1=ALU.mult,
            )
        for gid in range(4):
            ep_tanh(gid)
            ep_w(gid)

        consume_tile(4)
        consume_tile(5)
        for gid in (4, 5):
            ep_add(gid)
            ep_tanh(gid)
        for gid in (4, 5):
            ep_out(gid)
        consume_tile(6)
        ep_add(6)
        ep_tanh(6)
        ep_out(6)
        for j in range(3):
            consume_dma(7, j)
        ep_add(7)
        ep_tanh(7)
        consume_dma(7, 3)
        ep_add(8)
        ep_tanh(8)
        ep_out(7)
        ep_out(8)
